import numpy as np
import ml_dtypes


def mxq(x, axis, fmt="e4m3"):
    dtype, down = {"e4m3": (ml_dtypes.float8_e4m3fn, 7), "e5m2": (ml_dtypes.float8_e5m2, 14)}[fmt]
    v = np.moveaxis(np.asarray(x, np.float32).astype(ml_dtypes.bfloat16).astype(np.float64), axis, -1)
    blocks = v.reshape(v.shape[:-1] + (-1, 32))
    amax = np.abs(blocks).max(-1, keepdims=True)
    byte = np.maximum(np.where(amax > 0, np.frexp(amax)[1] - 1 + 127, 0) - down, 1)
    scale = np.exp2(byte - 127.0)
    codes = (blocks / scale).astype(np.float32).astype(dtype).astype(np.float64)
    return np.moveaxis((codes * scale).reshape(v.shape), -1, axis)


WIDE = False


def mx_kscale(k):
    if not WIDE:
        return np.ones(k)
    levels = np.array([10, -10, 5, -5, 0])
    a = np.random.permutation(np.resize(levels, k // 512 * 4)).reshape(k // 512, 4)
    idx = np.arange(k)
    return np.exp2(a[idx // 512, idx % 128 // 32])


BF16 = ml_dtypes.bfloat16


def bf(x):
    return np.asarray(x, np.float32).astype(BF16)


def f64(x):
    return np.asarray(x).astype(np.float64)


B, C_IN, H, W, C_OUT = 2, 512, 64, 64, 512


def _box_sum(x):
    b, h, w, c = x.shape
    xp = np.pad(x, ((0, 0), (1, 1), (1, 1), (0, 0)))
    out = np.zeros_like(x)
    for i in range(3):
        for j in range(3):
            out = out + xp[:, i:i + h, j:j + w, :]
    return out


def setup_inputs():
    s = mx_kscale(C_IN)
    return {"x": bf(np.random.standard_normal((B, C_IN, H, W)) * s[None, :, None, None]),
            "weight": bf(np.random.standard_normal((1, C_IN, C_OUT)) * 3.0 / np.sqrt(C_IN) / s[None, :, None])}


def reference(x, weight):
    x = f64(x)
    weight = f64(weight)
    b, c, h, w = x.shape
    o = weight.shape[-1]
    x1 = np.transpose(x, (0, 2, 3, 1))
    xw = mxq(x1, 3, "e4m3") @ mxq(weight[0], 0, "e4m3")
    deg = _box_sum(np.ones((1, h, w, 1)))
    dinv = 1.0 / np.sqrt(deg)
    y = dinv * _box_sum(dinv * xw)
    return np.transpose(y, (0, 3, 1, 2)).reshape(b, o, w, h)

@@ -1,0 +1,166 @@
+from contextlib import ExitStack
+import math
+
+import concourse.mybir as mybir
+
+F32 = mybir.dt.float32
+BF16 = mybir.dt.bfloat16
+U32 = mybir.dt.uint32
+U8 = mybir.dt.uint8
+I32 = mybir.dt.int32
+FP8X4 = mybir.dt.float8_e4m3fn_x4
+ADD = mybir.AluOpType.add
+COPY = mybir.ActivationFunctionType.Copy
+
+P = 128
+B, C_IN, H, W, C_OUT = 2, 512, 64, 64, 512
+FLOPS = 2 * B * H * W * C_IN * C_OUT
+PIX = H * W
+UNIT_ROWS = 8
+UNIT = UNIT_ROWS * W
+UNITS = PIX // UNIT
+CHUNK = 2 * UNIT
+SLOT = 68
+RHO = math.sqrt(1.5)
+NINTH = 1.0 / 9.0
+V_SHARE = 192
+
+
+def tile_gcn_layer_kernel(tc, x, weight, out):
+    nc = tc.nc
+    with ExitStack() as ctx:
+        keep = ctx.enter_context(tc.tile_pool(name="keep", bufs=1))
+        rawp = ctx.enter_context(tc.tile_pool(name="rawp", bufs=8))
+        grpp = ctx.enter_context(tc.tile_pool(name="grpp", bufs=4))
+        pairp = ctx.enter_context(tc.tile_pool(name="pairp", bufs=2))
+        edgep = ctx.enter_context(tc.tile_pool(name="edgep", bufs=2))
+        outp = ctx.enter_context(tc.tile_pool(name="outp", bufs=4))
+        psum = ctx.enter_context(tc.psum_pool(name="psum", bufs=7))
+        psume = ctx.enter_context(tc.psum_pool(name="psume", bufs=1))
+
+        w_raw = keep.tile([P, 4, C_OUT], BF16, name="w_raw")
+        nc.sync.dma_start(out=w_raw[:], in_=weight[0].rearrange("(p t) o -> p t o", t=4))
+        raws = []
+        for b in range(B):
+            xb = x[b].rearrange("(p t) i j -> p t (i j)", t=4)
+            for ch in range(PIX // CHUNK):
+                raw = rawp.tile([P, 4, CHUNK], BF16, name="raw")
+                nc.sync.dma_start(out=raw[:], in_=xb[:, :, ch * CHUNK:(ch + 1) * CHUNK])
+                raws.append(raw)
+
+        t_tiles = []
+        for k in range(3):
+            t_tile = keep.tile([P, 2, 16, SLOT], F32, name="t_tile%d" % k)
+            nc.vector.memset(t_tile[:], 0.0)
+            t_tiles.append(t_tile)
+        codes = []
+        scales = []
+        for b in range(B):
+            cd = keep.tile([P, PIX + 2 * W], U32, name="codes%d" % b, align_bytes=64)
+            sc = keep.tile([P, PIX + 2 * W], U8, name="scales%d" % b, align_bytes=64)
+            for lo in (0, PIX + W):
+                nc.vector.memset(cd[:, lo:lo + W].bitcast(I32), 0)
+                nc.vector.memset(sc[:, lo:lo + W].bitcast(I32), 0)
+            codes.append(cd)
+            scales.append(sc)
+
+        w_grp = keep.tile([P, C_OUT, 4], BF16, name="w_grp", align_bytes=64)
+        nc.vector.tensor_copy(
+            out=w_grp[:].rearrange("p (c i) t -> p c t i", i=4),
+            in_=w_raw[:].rearrange("p t (c i) -> p c t i", i=4),
+        )
+        w_codes = keep.tile([P, C_OUT], U32, name="w_codes", align_bytes=64)
+        w_scales = keep.tile([P, C_OUT], U8, name="w_scales", align_bytes=64)
+        nc.vector.quantize_mx(
+            out=w_codes[:].bitcast(FP8X4),
+            scales=w_scales[:],
+            in_=w_grp[:].rearrange("p w t -> p (w t)"),
+        )
+
+        def prep(gu):
+            b, u = divmod(gu, UNITS)
+            src = raws[gu // 2][:, :, (gu % 2) * UNIT:(gu % 2 + 1) * UNIT]
+            grouped = grpp.tile([P, UNIT, 4], BF16, name="grouped", align_bytes=64)
+            nc.vector.tensor_copy(
+                out=grouped[:, 0:V_SHARE, :].rearrange("p (c i) t -> p c t i", i=4),
+                in_=src[:, :, 0:V_SHARE].rearrange("p t (c i) -> p c t i", i=4),
+            )
+            nc.scalar.copy(
+                out=grouped[:, V_SHARE:UNIT, :].rearrange("p (c i) t -> p c t i", i=4),
+                in_=src[:, :, V_SHARE:UNIT].rearrange("p t (c i) -> p c t i", i=4),
+            )
+            lo = W + u * UNIT
+            nc.vector.quantize_mx(
+                out=codes[b][:, lo:lo + UNIT].bitcast(FP8X4),
+                scales=scales[b][:, lo:lo + UNIT],
+                in_=grouped[:].rearrange("p w t -> p (w t)"),
+            )
+
+        def mx(acc, b, oc, lo, n, start, stop):
+            nc.tensor.matmul_mx(
+                out=acc,
+                lhsT=w_codes[:, oc * P:(oc + 1) * P].bitcast(FP8X4),
+                lhsT_scale=w_scales[:, oc * P:(oc + 1) * P],
+                rhs=codes[b][:, lo:lo + n].bitcast(FP8X4),
+                rhs_scale=scales[b][:, lo:lo + n],
+                start=start,
+                stop=stop,
+            )
+
+        ready = 0
+        n_group = 0
+        for b in range(B):
+            ob = out[b].rearrange("(q p) i j -> p q (i j)", p=P)
+            for rb in range(4):
+                for op in range(2):
+                    want = min(B * UNITS, n_group + 5)
+                    while ready < want:
+                        prep(ready)
+                        ready += 1
+                    t_tile = t_tiles[n_group % 3]
+                    t_rows = t_tile[:].rearrange("p q r c -> p (q r) c")
+                    for h in range(2):
+                        for q in range(2):
+                            acc = psum.tile([P, UNIT], F32, name="acc")
+                            i0 = rb * 16 + h * UNIT_ROWS
+                            for k, d in enumerate((0, -1, 1)):
+                                mx(acc[:], b, 2 * op + q, W * (i0 + d + 1), UNIT, k == 0, k == 2)
+                            av = acc[:].rearrange("p (r m e) -> p r m e", m=32, e=2)
+                            dst = t_tile[:, q, h * UNIT_ROWS:(h + 1) * UNIT_ROWS, :]
+                            nc.scalar.activation(out=dst[:, :, 1:33], in_=av[:, :, :, 1], func=COPY, scale=NINTH)
+                            nc.scalar.activation(out=dst[:, :, 33:65], in_=av[:, :, :, 0], func=COPY, scale=NINTH)
+                    nc.scalar.activation(out=t_rows[:, :, 32:34], in_=t_rows[:, :, 32:34], func=COPY, scale=RHO)
+                    if rb in (0, 3):
+                        side = 0 if rb == 0 else 1
+                        eps = psume.tile([P, UNIT], F32, name="eps")
+                        for q in range(2):
+                            mx(eps[:, q * P:(q + 1) * P], b, 2 * op + q, W * (1 + side * 62), P, True, True)
+                        ev = eps[:, 0:2 * P].rearrange("p (q s m e) -> p q s m e", q=2, s=2, m=32, e=2)
+                        t_edge = edgep.tile([P, 2, SLOT], F32, name="t_edge")
+                        cc = (RHO - 1.0) * NINTH
+                        nc.scalar.activation(out=t_edge[:, :, 1:33], in_=ev[:, :, side, :, 1], func=COPY, scale=cc)
+                        nc.scalar.activation(out=t_edge[:, :, 33:65], in_=ev[:, :, side, :, 0], func=COPY, scale=cc)
+                        nc.scalar.activation(out=t_edge[:, :, 32:34], in_=t_edge[:, :, 32:34], func=COPY, scale=RHO)
+                        r0 = 14 * side
+                        nc.vector.tensor_tensor(
+                            out=t_tile[:, :, r0:r0 + 2, 1:65],
+                            in0=t_tile[:, :, r0:r0 + 2, 1:65],
+                            in1=t_edge[:, :, 1:65].unsqueeze(2).to_broadcast([P, 2, 2, 64]),
+                            op=ADD,
+                        )
+                    pair = pairp.tile([P, 32, 32], F32, name="pair")
+                    nc.vector.tensor_tensor(out=pair[:], in0=t_rows[:, :, 33:65], in1=t_rows[:, :, 1:33], op=ADD)
+                    y_tile = outp.tile([P, 2, 16 * W], F32, name="y_tile")
+                    nc.vector.tensor_tensor(
+                        out=y_tile[:].rearrange("p q (r m e) -> p (q r) m e", m=32, e=2),
+                        in0=t_rows[:].rearrange("p r (e y) -> p r y e", e=2)[:, :, 0:32, :],
+                        in1=pair[:].unsqueeze(3).to_broadcast([P, 32, 32, 2]),
+                        op=ADD,
+                    )
+                    y_rows = y_tile[:].rearrange("p q (r j) -> p (q r) j", j=W)
+                    nc.scalar.activation(out=y_rows[:, :, 0:W:W - 1], in_=y_rows[:, :, 0:W:W - 1], func=COPY, scale=RHO)
+                    if rb in (0, 3):
+                        lo = 0 if rb == 0 else 15 * W
+                        nc.scalar.activation(out=y_tile[:, :, lo:lo + W], in_=y_tile[:, :, lo:lo + W], func=COPY, scale=RHO)
+                    nc.sync.dma_start(out=ob[:, 2 * op:2 * op + 2, rb * 16 * W:(rb + 1) * 16 * W], in_=y_tile[:])
+                    n_group += 1

@@ -10,6 +10,7 @@ U8 = mybir.dt.uint8
 I32 = mybir.dt.int32
 FP8X4 = mybir.dt.float8_e4m3fn_x4
 ADD = mybir.AluOpType.add
+MULT = mybir.AluOpType.mult
 COPY = mybir.ActivationFunctionType.Copy
 
 P = 128
@@ -19,11 +20,19 @@ PIX = H * W
 UNIT_ROWS = 8
 UNIT = UNIT_ROWS * W
 UNITS = PIX // UNIT
+N_UNITS = B * UNITS
 CHUNK = 2 * UNIT
 SLOT = 68
 RHO = math.sqrt(1.5)
 NINTH = 1.0 / 9.0
-V_SHARE = 192
+N_GROUPS = 16
+HEAD_UNITS = 3
+HEAD_SHARES = (256, 128)
+SHARES = (96, 224)
+RG_AHEAD = 6
+Q_AHEAD = 4
+W_SHARES = (256, 128)
+FINE_GROUPS = (0, 15)
 
 
 def tile_gcn_layer_kernel(tc, x, weight, out):
@@ -31,12 +40,13 @@ def tile_gcn_layer_kernel(tc, x, weight, out):
     with ExitStack() as ctx:
         keep = ctx.enter_context(tc.tile_pool(name="keep", bufs=1))
         rawp = ctx.enter_context(tc.tile_pool(name="rawp", bufs=8))
-        grpp = ctx.enter_context(tc.tile_pool(name="grpp", bufs=4))
+        grpp = ctx.enter_context(tc.tile_pool(name="grpp", bufs=5))
         pairp = ctx.enter_context(tc.tile_pool(name="pairp", bufs=2))
         edgep = ctx.enter_context(tc.tile_pool(name="edgep", bufs=2))
         outp = ctx.enter_context(tc.tile_pool(name="outp", bufs=4))
         psum = ctx.enter_context(tc.psum_pool(name="psum", bufs=7))
         psume = ctx.enter_context(tc.psum_pool(name="psume", bufs=1))
+
 
         w_raw = keep.tile([P, 4, C_OUT], BF16, name="w_raw")
         nc.sync.dma_start(out=w_raw[:], in_=weight[0].rearrange("(p t) o -> p t o", t=4))
@@ -45,13 +55,19 @@ def tile_gcn_layer_kernel(tc, x, weight, out):
             xb = x[b].rearrange("(p t) i j -> p t (i j)", t=4)
             for ch in range(PIX // CHUNK):
                 raw = rawp.tile([P, 4, CHUNK], BF16, name="raw")
-                nc.sync.dma_start(out=raw[:], in_=xb[:, :, ch * CHUNK:(ch + 1) * CHUNK])
+                if b == 0 and ch == 0:
+                    for hh in range(2):
+                        nc.sync.dma_start(out=raw[:, :, hh * UNIT:(hh + 1) * UNIT], in_=xb[:, :, hh * UNIT:(hh + 1) * UNIT])
+                else:
+                    nc.sync.dma_start(out=raw[:], in_=xb[:, :, ch * CHUNK:(ch + 1) * CHUNK])
                 raws.append(raw)
 
         t_tiles = []
         for k in range(3):
             t_tile = keep.tile([P, 2, 16, SLOT], F32, name="t_tile%d" % k)
-            nc.vector.memset(t_tile[:], 0.0)
+            t_flat = t_tile[:].rearrange("p q r c -> p (q r) c")
+            nc.vector.memset(t_flat[:, :, 0:8], 0.0)
+            nc.vector.memset(t_flat[:, :, SLOT - 8:SLOT], 0.0)
             t_tiles.append(t_tile)
         codes = []
         scales = []
@@ -64,36 +80,50 @@ def tile_gcn_layer_kernel(tc, x, weight, out):
             codes.append(cd)
             scales.append(sc)
 
+        def interleave(dst, src, shares):
+            width = dst.shape[1]
+            v_px, s_px = shares
+            cut = v_px + s_px
+            if v_px > 0:
+                nc.vector.tensor_copy(
+                    out=dst[:, 0:v_px, :].rearrange("p (c i) t -> p c t i", i=4),
+                    in_=src[:, :, 0:v_px].rearrange("p t (c i) -> p c t i", i=4),
+                )
+            if s_px > 0:
+                nc.scalar.copy(
+                    out=dst[:, v_px:cut, :].rearrange("p (c i) t -> p c t i", i=4),
+                    in_=src[:, :, v_px:cut].rearrange("p t (c i) -> p c t i", i=4),
+                )
+            if cut < width:
+                nc.gpsimd.tensor_scalar(
+                    out=dst[:, cut:width, :],
+                    in0=src[:, :, cut:width].rearrange("p t w -> p w t"),
+                    scalar1=1.0,
+                    scalar2=0.0,
+                    op0=MULT,
+                    op1=ADD,
+                )
+
         w_grp = keep.tile([P, C_OUT, 4], BF16, name="w_grp", align_bytes=64)
-        nc.vector.tensor_copy(
-            out=w_grp[:].rearrange("p (c i) t -> p c t i", i=4),
-            in_=w_raw[:].rearrange("p t (c i) -> p c t i", i=4),
-        )
+        interleave(w_grp, w_raw, W_SHARES)
         w_codes = keep.tile([P, C_OUT], U32, name="w_codes", align_bytes=64)
         w_scales = keep.tile([P, C_OUT], U8, name="w_scales", align_bytes=64)
-        nc.vector.quantize_mx(
-            out=w_codes[:].bitcast(FP8X4),
-            scales=w_scales[:],
-            in_=w_grp[:].rearrange("p w t -> p (w t)"),
-        )
 
-        def prep(gu):
-            b, u = divmod(gu, UNITS)
+        grouped_of = {}
+
+        def regroup(gu):
             src = raws[gu // 2][:, :, (gu % 2) * UNIT:(gu % 2 + 1) * UNIT]
             grouped = grpp.tile([P, UNIT, 4], BF16, name="grouped", align_bytes=64)
-            nc.vector.tensor_copy(
-                out=grouped[:, 0:V_SHARE, :].rearrange("p (c i) t -> p c t i", i=4),
-                in_=src[:, :, 0:V_SHARE].rearrange("p t (c i) -> p c t i", i=4),
-            )
-            nc.scalar.copy(
-                out=grouped[:, V_SHARE:UNIT, :].rearrange("p (c i) t -> p c t i", i=4),
-                in_=src[:, :, V_SHARE:UNIT].rearrange("p t (c i) -> p c t i", i=4),
-            )
+            interleave(grouped, src, HEAD_SHARES if gu < HEAD_UNITS else SHARES)
+            grouped_of[gu] = grouped
+
+        def quantise(gu):
+            b, u = divmod(gu, UNITS)
             lo = W + u * UNIT
             nc.vector.quantize_mx(
                 out=codes[b][:, lo:lo + UNIT].bitcast(FP8X4),
                 scales=scales[b][:, lo:lo + UNIT],
-                in_=grouped[:].rearrange("p w t -> p (w t)"),
+                in_=grouped_of[gu][:].rearrange("p w t -> p (w t)"),
             )
 
         def mx(acc, b, oc, lo, n, start, stop):
@@ -107,60 +137,151 @@ def tile_gcn_layer_kernel(tc, x, weight, out):
                 stop=stop,
             )
 
-        ready = 0
-        n_group = 0
-        for b in range(B):
+        def where(n):
+            b, rest = divmod(n, 8)
+            rb, op = divmod(rest, 2)
+            return b, rb, op
+
+        edge_of = {}
+        y_of = {}
+
+        def bank(n, q, h):
+            b, rb, op = where(n)
+            acc = psum.tile([P, UNIT], F32, name="acc")
+            i0 = rb * 16 + h * UNIT_ROWS
+            for k, d in enumerate((0, -1, 1)):
+                mx(acc[:], b, 2 * op + q, W * (i0 + d + 1), UNIT, k == 0, k == 2)
+            av = acc[:].rearrange("p (r m e) -> p r m e", m=32, e=2)
+            dst = t_tiles[n % 3][:, q, h * UNIT_ROWS:(h + 1) * UNIT_ROWS, :]
+            nc.scalar.activation(out=dst[:, :, 1:33], in_=av[:, :, :, 1], func=COPY, scale=NINTH)
+            nc.scalar.activation(out=dst[:, :, 33:65], in_=av[:, :, :, 0], func=COPY, scale=NINTH)
+
+        def border_row(n):
+            b, rb, op = where(n)
+            side = 0 if rb == 0 else 1
+            eps = psume.tile([P, UNIT], F32, name="eps")
+            for q in range(2):
+                mx(eps[:, q * P:(q + 1) * P], b, 2 * op + q, W * (1 + side * 62), P, True, True)
+            ev = eps[:, 0:2 * P].rearrange("p (q s m e) -> p q s m e", q=2, s=2, m=32, e=2)
+            t_edge = edgep.tile([P, 2, SLOT], F32, name="t_edge")
+            cc = (RHO - 1.0) * NINTH
+            nc.scalar.activation(out=t_edge[:, :, 1:33], in_=ev[:, :, side, :, 1], func=COPY, scale=cc)
+            nc.scalar.activation(out=t_edge[:, :, 33:65], in_=ev[:, :, side, :, 0], func=COPY, scale=cc)
+            nc.scalar.activation(out=t_edge[:, :, 32:34], in_=t_edge[:, :, 32:34], func=COPY, scale=RHO)
+            edge_of[n] = t_edge
+
+        def weigh_ends(n, lo, hi):
+            rows = t_tiles[n % 3][:].rearrange("p q r c -> p (q r) c")[:, lo:hi, 32:34]
+            nc.scalar.activation(out=rows, in_=rows, func=COPY, scale=RHO)
+
+        def add_border(n, q_lo, q_hi):
+            b, rb, op = where(n)
+            r0 = 0 if rb == 0 else 14
+            t_tile = t_tiles[n % 3]
+            nc.vector.tensor_tensor(
+                out=t_tile[:, q_lo:q_hi, r0:r0 + 2, 1:65],
+                in0=t_tile[:, q_lo:q_hi, r0:r0 + 2, 1:65],
+                in1=edge_of[n][:, q_lo:q_hi, 1:65].unsqueeze(2).to_broadcast([P, q_hi - q_lo, 2, 64]),
+                op=ADD,
+            )
+
+        def sum_rows(n, lo, hi):
+            t_rows = t_tiles[n % 3][:].rearrange("p q r c -> p (q r) c")[:, lo:hi, :]
+            pair = pairp.tile([P, hi - lo, 32], F32, name="pair%d" % (hi - lo))
+            nc.vector.tensor_tensor(out=pair[:], in0=t_rows[:, :, 33:65], in1=t_rows[:, :, 1:33], op=ADD)
+            nc.vector.tensor_tensor(
+                out=y_of[n][:].rearrange("p q (r m e) -> p (q r) m e", m=32, e=2)[:, lo:hi, :, :],
+                in0=t_rows.rearrange("p r (e y) -> p r y e", e=2)[:, :, 0:32, :],
+                in1=pair[:].unsqueeze(3).to_broadcast([P, hi - lo, 32, 2]),
+                op=ADD,
+            )
+
+        def scale_ends(n, lo, hi):
+            ends = y_of[n][:].rearrange("p q (r j) -> p (q r) j", j=W)[:, lo:hi, 0:W:W - 1]
+            nc.scalar.activation(out=ends, in_=ends, func=COPY, scale=RHO)
+
+        def scale_border(n, q_lo, q_hi):
+            b, rb, op = where(n)
+            lo = 0 if rb == 0 else 15 * W
+            row = y_of[n][:, q_lo:q_hi, lo:lo + W]
+            nc.scalar.activation(out=row, in_=row, func=COPY, scale=RHO)
+
+        def store(n, q_lo, q_hi, r_lo, r_hi):
+            b, rb, op = where(n)
             ob = out[b].rearrange("(q p) i j -> p q (i j)", p=P)
-            for rb in range(4):
-                for op in range(2):
-                    want = min(B * UNITS, n_group + 5)
-                    while ready < want:
-                        prep(ready)
-                        ready += 1
-                    t_tile = t_tiles[n_group % 3]
-                    t_rows = t_tile[:].rearrange("p q r c -> p (q r) c")
-                    for h in range(2):
-                        for q in range(2):
-                            acc = psum.tile([P, UNIT], F32, name="acc")
-                            i0 = rb * 16 + h * UNIT_ROWS
-                            for k, d in enumerate((0, -1, 1)):
-                                mx(acc[:], b, 2 * op + q, W * (i0 + d + 1), UNIT, k == 0, k == 2)
-                            av = acc[:].rearrange("p (r m e) -> p r m e", m=32, e=2)
-                            dst = t_tile[:, q, h * UNIT_ROWS:(h + 1) * UNIT_ROWS, :]
-                            nc.scalar.activation(out=dst[:, :, 1:33], in_=av[:, :, :, 1], func=COPY, scale=NINTH)
-                            nc.scalar.activation(out=dst[:, :, 33:65], in_=av[:, :, :, 0], func=COPY, scale=NINTH)
-                    nc.scalar.activation(out=t_rows[:, :, 32:34], in_=t_rows[:, :, 32:34], func=COPY, scale=RHO)
-                    if rb in (0, 3):
-                        side = 0 if rb == 0 else 1
-                        eps = psume.tile([P, UNIT], F32, name="eps")
-                        for q in range(2):
-                            mx(eps[:, q * P:(q + 1) * P], b, 2 * op + q, W * (1 + side * 62), P, True, True)
-                        ev = eps[:, 0:2 * P].rearrange("p (q s m e) -> p q s m e", q=2, s=2, m=32, e=2)
-                        t_edge = edgep.tile([P, 2, SLOT], F32, name="t_edge")
-                        cc = (RHO - 1.0) * NINTH
-                        nc.scalar.activation(out=t_edge[:, :, 1:33], in_=ev[:, :, side, :, 1], func=COPY, scale=cc)
-                        nc.scalar.activation(out=t_edge[:, :, 33:65], in_=ev[:, :, side, :, 0], func=COPY, scale=cc)
-                        nc.scalar.activation(out=t_edge[:, :, 32:34], in_=t_edge[:, :, 32:34], func=COPY, scale=RHO)
-                        r0 = 14 * side
-                        nc.vector.tensor_tensor(
-                            out=t_tile[:, :, r0:r0 + 2, 1:65],
-                            in0=t_tile[:, :, r0:r0 + 2, 1:65],
-                            in1=t_edge[:, :, 1:65].unsqueeze(2).to_broadcast([P, 2, 2, 64]),
-                            op=ADD,
-                        )
-                    pair = pairp.tile([P, 32, 32], F32, name="pair")
-                    nc.vector.tensor_tensor(out=pair[:], in0=t_rows[:, :, 33:65], in1=t_rows[:, :, 1:33], op=ADD)
-                    y_tile = outp.tile([P, 2, 16 * W], F32, name="y_tile")
-                    nc.vector.tensor_tensor(
-                        out=y_tile[:].rearrange("p q (r m e) -> p (q r) m e", m=32, e=2),
-                        in0=t_rows[:].rearrange("p r (e y) -> p r y e", e=2)[:, :, 0:32, :],
-                        in1=pair[:].unsqueeze(3).to_broadcast([P, 32, 32, 2]),
-                        op=ADD,
-                    )
-                    y_rows = y_tile[:].rearrange("p q (r j) -> p (q r) j", j=W)
-                    nc.scalar.activation(out=y_rows[:, :, 0:W:W - 1], in_=y_rows[:, :, 0:W:W - 1], func=COPY, scale=RHO)
-                    if rb in (0, 3):
-                        lo = 0 if rb == 0 else 15 * W
-                        nc.scalar.activation(out=y_tile[:, :, lo:lo + W], in_=y_tile[:, :, lo:lo + W], func=COPY, scale=RHO)
-                    nc.sync.dma_start(out=ob[:, 2 * op:2 * op + 2, rb * 16 * W:(rb + 1) * 16 * W], in_=y_tile[:])
-                    n_group += 1
+            nc.sync.dma_start(
+                out=ob[:, 2 * op + q_lo:2 * op + q_hi, (rb * 16 + r_lo) * W:(rb * 16 + r_hi) * W],
+                in_=y_of[n][:, q_lo:q_hi, r_lo * W:r_hi * W],
+            )
+
+        def new_y(n):
+            y_tile = outp.tile([P, 2, 16 * W], F32, name="y_tile")
+            y_of[n] = y_tile
+
+        def fine_group(n):
+            b, rb, op = where(n)
+            new_y(n)
+            border_row(n)
+            h_border = 0 if rb == 0 else 1
+            for h in range(2):
+                for q in range(2):
+                    lo = q * 16 + h * UNIT_ROWS
+                    bank(n, q, h)
+                    weigh_ends(n, lo, lo + UNIT_ROWS)
+                    if h == h_border:
+                        add_border(n, q, q + 1)
+                    sum_rows(n, lo, lo + UNIT_ROWS)
+                    scale_ends(n, lo, lo + UNIT_ROWS)
+                    if h == h_border:
+                        scale_border(n, q, q + 1)
+                    store(n, q, q + 1, h * UNIT_ROWS, (h + 1) * UNIT_ROWS)
+
+        def multiply_and_empty(n):
+            b, rb, op = where(n)
+            for h in range(2):
+                for q in range(2):
+                    bank(n, q, h)
+            weigh_ends(n, 0, 32)
+            if rb in (0, 3):
+                border_row(n)
+
+        def add_up(n):
+            b, rb, op = where(n)
+            if rb in (0, 3):
+                add_border(n, 0, 2)
+            new_y(n)
+            sum_rows(n, 0, 32)
+
+        def finish(n):
+            b, rb, op = where(n)
+            scale_ends(n, 0, 32)
+            if rb in (0, 3):
+                scale_border(n, 0, 2)
+            store(n, 0, 2, 0, 16)
+
+        regroup(0)
+        nc.vector.quantize_mx(
+            out=w_codes[:].bitcast(FP8X4),
+            scales=w_scales[:],
+            in_=w_grp[:].rearrange("p w t -> p (w t)"),
+        )
+        for gu in range(1, RG_AHEAD):
+            regroup(gu)
+            if gu - 1 < Q_AHEAD:
+                quantise(gu - 1)
+        for gu in range(RG_AHEAD - 1, Q_AHEAD):
+            quantise(gu)
+        for n in range(N_GROUPS + 1):
+            if n < N_GROUPS:
+                if n in FINE_GROUPS:
+                    fine_group(n)
+                else:
+                    multiply_and_empty(n)
+            if n + RG_AHEAD < N_UNITS:
+                regroup(n + RG_AHEAD)
+            if n >= 1 and n - 1 not in FINE_GROUPS:
+                add_up(n - 1)
+            if n + Q_AHEAD < N_UNITS:
+                quantise(n + Q_AHEAD)
+            if n >= 1 and n - 1 not in FINE_GROUPS:
+                finish(n - 1)

@@ -26,12 +26,12 @@ SLOT = 68
 RHO = math.sqrt(1.5)
 NINTH = 1.0 / 9.0
 N_GROUPS = 16
-HEAD_UNITS = 3
-HEAD_SHARES = (256, 128)
-SHARES = (96, 224)
-RG_AHEAD = 6
-Q_AHEAD = 4
-W_SHARES = (256, 128)
+HEAD_UNITS = 0
+HEAD_SHARES = (256, 256)
+SHARES = (224, 288)
+RG_AHEAD = 8
+Q_AHEAD = 6
+W_SHARES = (320, 192)
 FINE_GROUPS = (0, 15)
 
 

@@ -28,7 +28,7 @@ NINTH = 1.0 / 9.0
 N_GROUPS = 16
 HEAD_UNITS = 0
 HEAD_SHARES = (256, 256)
-SHARES = (224, 288)
+SHARES = (288, 224)
 RG_AHEAD = 8
 Q_AHEAD = 6
 W_SHARES = (320, 192)

@@ -28,11 +28,11 @@ NINTH = 1.0 / 9.0
 N_GROUPS = 16
 HEAD_UNITS = 0
 HEAD_SHARES = (256, 256)
-SHARES = (288, 224)
+SHARES = (272, 240)
 RG_AHEAD = 8
 Q_AHEAD = 6
 W_SHARES = (320, 192)
-FINE_GROUPS = (0, 15)
+FINE_GROUPS = (99,)
 
 
 def tile_gcn_layer_kernel(tc, x, weight, out):

@@ -32,7 +32,7 @@ SHARES = (272, 240)
 RG_AHEAD = 8
 Q_AHEAD = 6
 W_SHARES = (320, 192)
-FINE_GROUPS = (99,)
+FINE_GROUPS = (0, 15)
 
 
 def tile_gcn_layer_kernel(tc, x, weight, out):
@@ -41,9 +41,9 @@ def tile_gcn_layer_kernel(tc, x, weight, out):
         keep = ctx.enter_context(tc.tile_pool(name="keep", bufs=1))
         rawp = ctx.enter_context(tc.tile_pool(name="rawp", bufs=8))
         grpp = ctx.enter_context(tc.tile_pool(name="grpp", bufs=5))
-        pairp = ctx.enter_context(tc.tile_pool(name="pairp", bufs=2))
+        pairp = ctx.enter_context(tc.tile_pool(name="pairp", bufs=3))
         edgep = ctx.enter_context(tc.tile_pool(name="edgep", bufs=2))
-        outp = ctx.enter_context(tc.tile_pool(name="outp", bufs=4))
+        outp = ctx.enter_context(tc.tile_pool(name="outp", bufs=5))
         psum = ctx.enter_context(tc.psum_pool(name="psum", bufs=7))
         psume = ctx.enter_context(tc.psum_pool(name="psume", bufs=1))
 
@@ -63,7 +63,7 @@ def tile_gcn_layer_kernel(tc, x, weight, out):
                 raws.append(raw)
 
         t_tiles = []
-        for k in range(3):
+        for k in range(4):
             t_tile = keep.tile([P, 2, 16, SLOT], F32, name="t_tile%d" % k)
             t_flat = t_tile[:].rearrange("p q r c -> p (q r) c")
             nc.vector.memset(t_flat[:, :, 0:8], 0.0)
@@ -152,7 +152,7 @@ def tile_gcn_layer_kernel(tc, x, weight, out):
             for k, d in enumerate((0, -1, 1)):
                 mx(acc[:], b, 2 * op + q, W * (i0 + d + 1), UNIT, k == 0, k == 2)
             av = acc[:].rearrange("p (r m e) -> p r m e", m=32, e=2)
-            dst = t_tiles[n % 3][:, q, h * UNIT_ROWS:(h + 1) * UNIT_ROWS, :]
+            dst = t_tiles[n % 4][:, q, h * UNIT_ROWS:(h + 1) * UNIT_ROWS, :]
             nc.scalar.activation(out=dst[:, :, 1:33], in_=av[:, :, :, 1], func=COPY, scale=NINTH)
             nc.scalar.activation(out=dst[:, :, 33:65], in_=av[:, :, :, 0], func=COPY, scale=NINTH)
 
@@ -171,13 +171,13 @@ def tile_gcn_layer_kernel(tc, x, weight, out):
             edge_of[n] = t_edge
 
         def weigh_ends(n, lo, hi):
-            rows = t_tiles[n % 3][:].rearrange("p q r c -> p (q r) c")[:, lo:hi, 32:34]
+            rows = t_tiles[n % 4][:].rearrange("p q r c -> p (q r) c")[:, lo:hi, 32:34]
             nc.scalar.activation(out=rows, in_=rows, func=COPY, scale=RHO)
 
         def add_border(n, q_lo, q_hi):
             b, rb, op = where(n)
             r0 = 0 if rb == 0 else 14
-            t_tile = t_tiles[n % 3]
+            t_tile = t_tiles[n % 4]
             nc.vector.tensor_tensor(
                 out=t_tile[:, q_lo:q_hi, r0:r0 + 2, 1:65],
                 in0=t_tile[:, q_lo:q_hi, r0:r0 + 2, 1:65],
@@ -186,7 +186,7 @@ def tile_gcn_layer_kernel(tc, x, weight, out):
             )
 
         def sum_rows(n, lo, hi):
-            t_rows = t_tiles[n % 3][:].rearrange("p q r c -> p (q r) c")[:, lo:hi, :]
+            t_rows = t_tiles[n % 4][:].rearrange("p q r c -> p (q r) c")[:, lo:hi, :]
             pair = pairp.tile([P, hi - lo, 32], F32, name="pair%d" % (hi - lo))
             nc.vector.tensor_tensor(out=pair[:], in0=t_rows[:, :, 33:65], in1=t_rows[:, :, 1:33], op=ADD)
             nc.vector.tensor_tensor(

@@ -29,8 +29,8 @@ N_GROUPS = 16
 HEAD_UNITS = 0
 HEAD_SHARES = (256, 256)
 SHARES = (272, 240)
-RG_AHEAD = 8
-Q_AHEAD = 6
+RG_AHEAD = 7
+Q_AHEAD = 5
 W_SHARES = (320, 192)
 FINE_GROUPS = (0, 15)
 
@@ -64,7 +64,7 @@ def tile_gcn_layer_kernel(tc, x, weight, out):
 
         t_tiles = []
         for k in range(4):
-            t_tile = keep.tile([P, 2, 16, SLOT], F32, name="t_tile%d" % k)
+            t_tile = keep.tile([P, 4, UNIT_ROWS, SLOT], F32, name="t_tile%d" % k)
             t_flat = t_tile[:].rearrange("p q r c -> p (q r) c")
             nc.vector.memset(t_flat[:, :, 0:8], 0.0)
             nc.vector.memset(t_flat[:, :, SLOT - 8:SLOT], 0.0)
@@ -138,32 +138,30 @@ def tile_gcn_layer_kernel(tc, x, weight, out):
             )
 
         def where(n):
-            b, rest = divmod(n, 8)
-            rb, op = divmod(rest, 2)
-            return b, rb, op
+            return divmod(n, UNITS)
 
         edge_of = {}
         y_of = {}
 
-        def bank(n, q, h):
-            b, rb, op = where(n)
+        def bank(n, q):
+            b, u = where(n)
             acc = psum.tile([P, UNIT], F32, name="acc")
-            i0 = rb * 16 + h * UNIT_ROWS
+            i0 = u * UNIT_ROWS
             for k, d in enumerate((0, -1, 1)):
-                mx(acc[:], b, 2 * op + q, W * (i0 + d + 1), UNIT, k == 0, k == 2)
+                mx(acc[:], b, q, W * (i0 + d + 1), UNIT, k == 0, k == 2)
             av = acc[:].rearrange("p (r m e) -> p r m e", m=32, e=2)
-            dst = t_tiles[n % 4][:, q, h * UNIT_ROWS:(h + 1) * UNIT_ROWS, :]
+            dst = t_tiles[n % 4][:, q, :, :]
             nc.scalar.activation(out=dst[:, :, 1:33], in_=av[:, :, :, 1], func=COPY, scale=NINTH)
             nc.scalar.activation(out=dst[:, :, 33:65], in_=av[:, :, :, 0], func=COPY, scale=NINTH)
 
         def border_row(n):
-            b, rb, op = where(n)
-            side = 0 if rb == 0 else 1
+            b, u = where(n)
+            side = 0 if u == 0 else 1
             eps = psume.tile([P, UNIT], F32, name="eps")
-            for q in range(2):
-                mx(eps[:, q * P:(q + 1) * P], b, 2 * op + q, W * (1 + side * 62), P, True, True)
-            ev = eps[:, 0:2 * P].rearrange("p (q s m e) -> p q s m e", q=2, s=2, m=32, e=2)
-            t_edge = edgep.tile([P, 2, SLOT], F32, name="t_edge")
+            for q in range(4):
+                mx(eps[:, q * P:(q + 1) * P], b, q, W * (1 + side * 62), P, True, True)
+            ev = eps[:].rearrange("p (q s m e) -> p q s m e", q=4, s=2, m=32, e=2)
+            t_edge = edgep.tile([P, 4, SLOT], F32, name="t_edge")
             cc = (RHO - 1.0) * NINTH
             nc.scalar.activation(out=t_edge[:, :, 1:33], in_=ev[:, :, side, :, 1], func=COPY, scale=cc)
             nc.scalar.activation(out=t_edge[:, :, 33:65], in_=ev[:, :, side, :, 0], func=COPY, scale=cc)
@@ -175,8 +173,8 @@ def tile_gcn_layer_kernel(tc, x, weight, out):
             nc.scalar.activation(out=rows, in_=rows, func=COPY, scale=RHO)
 
         def add_border(n, q_lo, q_hi):
-            b, rb, op = where(n)
-            r0 = 0 if rb == 0 else 14
+            b, u = where(n)
+            r0 = 0 if u == 0 else UNIT_ROWS - 2
             t_tile = t_tiles[n % 4]
             nc.vector.tensor_tensor(
                 out=t_tile[:, q_lo:q_hi, r0:r0 + 2, 1:65],
@@ -201,63 +199,58 @@ def tile_gcn_layer_kernel(tc, x, weight, out):
             nc.scalar.activation(out=ends, in_=ends, func=COPY, scale=RHO)
 
         def scale_border(n, q_lo, q_hi):
-            b, rb, op = where(n)
-            lo = 0 if rb == 0 else 15 * W
+            b, u = where(n)
+            lo = 0 if u == 0 else (UNIT_ROWS - 1) * W
             row = y_of[n][:, q_lo:q_hi, lo:lo + W]
             nc.scalar.activation(out=row, in_=row, func=COPY, scale=RHO)
 
-        def store(n, q_lo, q_hi, r_lo, r_hi):
-            b, rb, op = where(n)
+        def store(n, q_lo, q_hi):
+            b, u = where(n)
             ob = out[b].rearrange("(q p) i j -> p q (i j)", p=P)
             nc.sync.dma_start(
-                out=ob[:, 2 * op + q_lo:2 * op + q_hi, (rb * 16 + r_lo) * W:(rb * 16 + r_hi) * W],
-                in_=y_of[n][:, q_lo:q_hi, r_lo * W:r_hi * W],
+                out=ob[:, q_lo:q_hi, u * UNIT:(u + 1) * UNIT],
+                in_=y_of[n][:, q_lo:q_hi, :],
             )
 
         def new_y(n):
-            y_tile = outp.tile([P, 2, 16 * W], F32, name="y_tile")
+            y_tile = outp.tile([P, 4, UNIT], F32, name="y_tile")
             y_of[n] = y_tile
 
         def fine_group(n):
-            b, rb, op = where(n)
+            b, u = where(n)
             new_y(n)
             border_row(n)
-            h_border = 0 if rb == 0 else 1
-            for h in range(2):
-                for q in range(2):
-                    lo = q * 16 + h * UNIT_ROWS
-                    bank(n, q, h)
-                    weigh_ends(n, lo, lo + UNIT_ROWS)
-                    if h == h_border:
-                        add_border(n, q, q + 1)
-                    sum_rows(n, lo, lo + UNIT_ROWS)
-                    scale_ends(n, lo, lo + UNIT_ROWS)
-                    if h == h_border:
-                        scale_border(n, q, q + 1)
-                    store(n, q, q + 1, h * UNIT_ROWS, (h + 1) * UNIT_ROWS)
+            for q in range(4):
+                lo = q * UNIT_ROWS
+                bank(n, q)
+                weigh_ends(n, lo, lo + UNIT_ROWS)
+                add_border(n, q, q + 1)
+                sum_rows(n, lo, lo + UNIT_ROWS)
+                scale_ends(n, lo, lo + UNIT_ROWS)
+                scale_border(n, q, q + 1)
+                store(n, q, q + 1)
 
         def multiply_and_empty(n):
-            b, rb, op = where(n)
-            for h in range(2):
-                for q in range(2):
-                    bank(n, q, h)
+            b, u = where(n)
+            for q in range(4):
+                bank(n, q)
             weigh_ends(n, 0, 32)
-            if rb in (0, 3):
+            if u in (0, UNITS - 1):
                 border_row(n)
 
         def add_up(n):
-            b, rb, op = where(n)
-            if rb in (0, 3):
-                add_border(n, 0, 2)
+            b, u = where(n)
+            if u in (0, UNITS - 1):
+                add_border(n, 0, 4)
             new_y(n)
             sum_rows(n, 0, 32)
 
         def finish(n):
-            b, rb, op = where(n)
+            b, u = where(n)
             scale_ends(n, 0, 32)
-            if rb in (0, 3):
-                scale_border(n, 0, 2)
-            store(n, 0, 2, 0, 16)
+            if u in (0, UNITS - 1):
+                scale_border(n, 0, 4)
+            store(n, 0, 4)
 
         regroup(0)
         nc.vector.quantize_mx(

@@ -28,7 +28,7 @@ NINTH = 1.0 / 9.0
 N_GROUPS = 16
 HEAD_UNITS = 0
 HEAD_SHARES = (256, 256)
-SHARES = (272, 240)
+SHARES = (256, 256)
 RG_AHEAD = 7
 Q_AHEAD = 5
 W_SHARES = (320, 192)
@@ -149,10 +149,9 @@ def tile_gcn_layer_kernel(tc, x, weight, out):
             i0 = u * UNIT_ROWS
             for k, d in enumerate((0, -1, 1)):
                 mx(acc[:], b, q, W * (i0 + d + 1), UNIT, k == 0, k == 2)
-            av = acc[:].rearrange("p (r m e) -> p r m e", m=32, e=2)
-            dst = t_tiles[n % 4][:, q, :, :]
-            nc.scalar.activation(out=dst[:, :, 1:33], in_=av[:, :, :, 1], func=COPY, scale=NINTH)
-            nc.scalar.activation(out=dst[:, :, 33:65], in_=av[:, :, :, 0], func=COPY, scale=NINTH)
+            av = acc[:].rearrange("p (r m e) -> p r e m", m=32, e=2)[:, :, ::-1, :]
+            dst = t_tiles[n % 4][:, q, :, 1:65].rearrange("p r (e m) -> p r e m", e=2)
+            nc.scalar.activation(out=dst, in_=av, func=COPY, scale=NINTH)
 
         def border_row(n):
             b, u = where(n)
@@ -160,11 +159,10 @@ def tile_gcn_layer_kernel(tc, x, weight, out):
             eps = psume.tile([P, UNIT], F32, name="eps")
             for q in range(4):
                 mx(eps[:, q * P:(q + 1) * P], b, q, W * (1 + side * 62), P, True, True)
-            ev = eps[:].rearrange("p (q s m e) -> p q s m e", q=4, s=2, m=32, e=2)
+            ev = eps[:].rearrange("p (q s m e) -> p q s e m", q=4, s=2, m=32, e=2)[:, :, side, ::-1, :]
             t_edge = edgep.tile([P, 4, SLOT], F32, name="t_edge")
             cc = (RHO - 1.0) * NINTH
-            nc.scalar.activation(out=t_edge[:, :, 1:33], in_=ev[:, :, side, :, 1], func=COPY, scale=cc)
-            nc.scalar.activation(out=t_edge[:, :, 33:65], in_=ev[:, :, side, :, 0], func=COPY, scale=cc)
+            nc.scalar.activation(out=t_edge[:, :, 1:65].rearrange("p q (e m) -> p q e m", e=2), in_=ev, func=COPY, scale=cc)
             nc.scalar.activation(out=t_edge[:, :, 32:34], in_=t_edge[:, :, 32:34], func=COPY, scale=RHO)
             edge_of[n] = t_edge
 

@@ -28,11 +28,13 @@ NINTH = 1.0 / 9.0
 N_GROUPS = 16
 HEAD_UNITS = 0
 HEAD_SHARES = (256, 256)
-SHARES = (256, 256)
+SHARES = (224, 288)
 RG_AHEAD = 7
 Q_AHEAD = 5
 W_SHARES = (320, 192)
 FINE_GROUPS = (0, 15)
+N_Y = 5
+Y_AT = 2
 
 
 def tile_gcn_layer_kernel(tc, x, weight, out):
@@ -43,7 +45,6 @@ def tile_gcn_layer_kernel(tc, x, weight, out):
         grpp = ctx.enter_context(tc.tile_pool(name="grpp", bufs=5))
         pairp = ctx.enter_context(tc.tile_pool(name="pairp", bufs=3))
         edgep = ctx.enter_context(tc.tile_pool(name="edgep", bufs=2))
-        outp = ctx.enter_context(tc.tile_pool(name="outp", bufs=5))
         psum = ctx.enter_context(tc.psum_pool(name="psum", bufs=7))
         psume = ctx.enter_context(tc.psum_pool(name="psume", bufs=1))
 
@@ -69,6 +70,12 @@ def tile_gcn_layer_kernel(tc, x, weight, out):
             nc.vector.memset(t_flat[:, :, 0:8], 0.0)
             nc.vector.memset(t_flat[:, :, SLOT - 8:SLOT], 0.0)
             t_tiles.append(t_tile)
+        y_tiles = []
+        for k in range(N_Y):
+            y_store = keep.tile([P, Y_AT - 1 + 33 * W], F32, name="y_store%d" % k)
+            nc.vector.memset(y_store[:, 0:Y_AT], 0.0)
+            nc.vector.memset(y_store[:, Y_AT + 4 * UNIT:Y_AT + 4 * UNIT + 2], 0.0)
+            y_tiles.append(y_store)
         codes = []
         scales = []
         for b in range(B):
@@ -186,14 +193,17 @@ def tile_gcn_layer_kernel(tc, x, weight, out):
             pair = pairp.tile([P, hi - lo, 32], F32, name="pair%d" % (hi - lo))
             nc.vector.tensor_tensor(out=pair[:], in0=t_rows[:, :, 33:65], in1=t_rows[:, :, 1:33], op=ADD)
             nc.vector.tensor_tensor(
-                out=y_of[n][:].rearrange("p q (r m e) -> p (q r) m e", m=32, e=2)[:, lo:hi, :, :],
+                out=y_of[n].rearrange("p q (r m e) -> p (q r) m e", m=32, e=2)[:, lo:hi, :, :],
                 in0=t_rows.rearrange("p r (e y) -> p r y e", e=2)[:, :, 0:32, :],
                 in1=pair[:].unsqueeze(3).to_broadcast([P, hi - lo, 32, 2]),
                 op=ADD,
             )
 
         def scale_ends(n, lo, hi):
-            ends = y_of[n][:].rearrange("p q (r j) -> p (q r) j", j=W)[:, lo:hi, 0:W:W - 1]
+            if hi - lo == 32:
+                ends = y_tiles[n % N_Y][:, Y_AT - 1:Y_AT - 1 + 33 * W].rearrange("p (k j) -> p k j", j=W)[:, :, 0:2]
+            else:
+                ends = y_of[n].rearrange("p q (r j) -> p (q r) j", j=W)[:, lo:hi, 0:W:W - 1]
             nc.scalar.activation(out=ends, in_=ends, func=COPY, scale=RHO)
 
         def scale_border(n, q_lo, q_hi):
@@ -211,8 +221,7 @@ def tile_gcn_layer_kernel(tc, x, weight, out):
             )
 
         def new_y(n):
-            y_tile = outp.tile([P, 4, UNIT], F32, name="y_tile")
-            y_of[n] = y_tile
+            y_of[n] = y_tiles[n % N_Y][:, Y_AT:Y_AT + 4 * UNIT].rearrange("p (q w) -> p q w", q=4)
 
         def fine_group(n):
             b, u = where(n)

@@ -28,7 +28,7 @@ NINTH = 1.0 / 9.0
 N_GROUPS = 16
 HEAD_UNITS = 0
 HEAD_SHARES = (256, 256)
-SHARES = (224, 288)
+SHARES = (240, 272)
 RG_AHEAD = 7
 Q_AHEAD = 5
 W_SHARES = (320, 192)

from contextlib import ExitStack
import math

import concourse.mybir as mybir

F32 = mybir.dt.float32
BF16 = mybir.dt.bfloat16
U32 = mybir.dt.uint32
U8 = mybir.dt.uint8
I32 = mybir.dt.int32
FP8X4 = mybir.dt.float8_e4m3fn_x4
ADD = mybir.AluOpType.add
MULT = mybir.AluOpType.mult
COPY = mybir.ActivationFunctionType.Copy

P = 128
B, C_IN, H, W, C_OUT = 2, 512, 64, 64, 512
FLOPS = 2 * B * H * W * C_IN * C_OUT
PIX = H * W
UNIT_ROWS = 8
UNIT = UNIT_ROWS * W
UNITS = PIX // UNIT
N_UNITS = B * UNITS
CHUNK = 2 * UNIT
SLOT = 68
RHO = math.sqrt(1.5)
NINTH = 1.0 / 9.0
N_GROUPS = 16
HEAD_UNITS = 0
HEAD_SHARES = (256, 256)
SHARES = (240, 272)
RG_AHEAD = 7
Q_AHEAD = 5
W_SHARES = (320, 192)
FINE_GROUPS = (0, 15)
N_Y = 5
Y_AT = 2


def tile_gcn_layer_kernel(tc, x, weight, out):
    nc = tc.nc
    with ExitStack() as ctx:
        keep = ctx.enter_context(tc.tile_pool(name="keep", bufs=1))
        rawp = ctx.enter_context(tc.tile_pool(name="rawp", bufs=8))
        grpp = ctx.enter_context(tc.tile_pool(name="grpp", bufs=5))
        pairp = ctx.enter_context(tc.tile_pool(name="pairp", bufs=3))
        edgep = ctx.enter_context(tc.tile_pool(name="edgep", bufs=2))
        psum = ctx.enter_context(tc.psum_pool(name="psum", bufs=7))
        psume = ctx.enter_context(tc.psum_pool(name="psume", bufs=1))


        w_raw = keep.tile([P, 4, C_OUT], BF16, name="w_raw")
        nc.sync.dma_start(out=w_raw[:], in_=weight[0].rearrange("(p t) o -> p t o", t=4))
        raws = []
        for b in range(B):
            xb = x[b].rearrange("(p t) i j -> p t (i j)", t=4)
            for ch in range(PIX // CHUNK):
                raw = rawp.tile([P, 4, CHUNK], BF16, name="raw")
                if b == 0 and ch == 0:
                    for hh in range(2):
                        nc.sync.dma_start(out=raw[:, :, hh * UNIT:(hh + 1) * UNIT], in_=xb[:, :, hh * UNIT:(hh + 1) * UNIT])
                else:
                    nc.sync.dma_start(out=raw[:], in_=xb[:, :, ch * CHUNK:(ch + 1) * CHUNK])
                raws.append(raw)

        t_tiles = []
        for k in range(4):
            t_tile = keep.tile([P, 4, UNIT_ROWS, SLOT], F32, name="t_tile%d" % k)
            t_flat = t_tile[:].rearrange("p q r c -> p (q r) c")
            nc.vector.memset(t_flat[:, :, 0:8], 0.0)
            nc.vector.memset(t_flat[:, :, SLOT - 8:SLOT], 0.0)
            t_tiles.append(t_tile)
        y_tiles = []
        for k in range(N_Y):
            y_store = keep.tile([P, Y_AT - 1 + 33 * W], F32, name="y_store%d" % k)
            nc.vector.memset(y_store[:, 0:Y_AT], 0.0)
            nc.vector.memset(y_store[:, Y_AT + 4 * UNIT:Y_AT + 4 * UNIT + 2], 0.0)
            y_tiles.append(y_store)
        codes = []
        scales = []
        for b in range(B):
            cd = keep.tile([P, PIX + 2 * W], U32, name="codes%d" % b, align_bytes=64)
            sc = keep.tile([P, PIX + 2 * W], U8, name="scales%d" % b, align_bytes=64)
            for lo in (0, PIX + W):
                nc.vector.memset(cd[:, lo:lo + W].bitcast(I32), 0)
                nc.vector.memset(sc[:, lo:lo + W].bitcast(I32), 0)
            codes.append(cd)
            scales.append(sc)

        def interleave(dst, src, shares):
            width = dst.shape[1]
            v_px, s_px = shares
            cut = v_px + s_px
            if v_px > 0:
                nc.vector.tensor_copy(
                    out=dst[:, 0:v_px, :].rearrange("p (c i) t -> p c t i", i=4),
                    in_=src[:, :, 0:v_px].rearrange("p t (c i) -> p c t i", i=4),
                )
            if s_px > 0:
                nc.scalar.copy(
                    out=dst[:, v_px:cut, :].rearrange("p (c i) t -> p c t i", i=4),
                    in_=src[:, :, v_px:cut].rearrange("p t (c i) -> p c t i", i=4),
                )
            if cut < width:
                nc.gpsimd.tensor_scalar(
                    out=dst[:, cut:width, :],
                    in0=src[:, :, cut:width].rearrange("p t w -> p w t"),
                    scalar1=1.0,
                    scalar2=0.0,
                    op0=MULT,
                    op1=ADD,
                )

        w_grp = keep.tile([P, C_OUT, 4], BF16, name="w_grp", align_bytes=64)
        interleave(w_grp, w_raw, W_SHARES)
        w_codes = keep.tile([P, C_OUT], U32, name="w_codes", align_bytes=64)
        w_scales = keep.tile([P, C_OUT], U8, name="w_scales", align_bytes=64)

        grouped_of = {}

        def regroup(gu):
            src = raws[gu // 2][:, :, (gu % 2) * UNIT:(gu % 2 + 1) * UNIT]
            grouped = grpp.tile([P, UNIT, 4], BF16, name="grouped", align_bytes=64)
            interleave(grouped, src, HEAD_SHARES if gu < HEAD_UNITS else SHARES)
            grouped_of[gu] = grouped

        def quantise(gu):
            b, u = divmod(gu, UNITS)
            lo = W + u * UNIT
            nc.vector.quantize_mx(
                out=codes[b][:, lo:lo + UNIT].bitcast(FP8X4),
                scales=scales[b][:, lo:lo + UNIT],
                in_=grouped_of[gu][:].rearrange("p w t -> p (w t)"),
            )

        def mx(acc, b, oc, lo, n, start, stop):
            nc.tensor.matmul_mx(
                out=acc,
                lhsT=w_codes[:, oc * P:(oc + 1) * P].bitcast(FP8X4),
                lhsT_scale=w_scales[:, oc * P:(oc + 1) * P],
                rhs=codes[b][:, lo:lo + n].bitcast(FP8X4),
                rhs_scale=scales[b][:, lo:lo + n],
                start=start,
                stop=stop,
            )

        def where(n):
            return divmod(n, UNITS)

        edge_of = {}
        y_of = {}

        def bank(n, q):
            b, u = where(n)
            acc = psum.tile([P, UNIT], F32, name="acc")
            i0 = u * UNIT_ROWS
            for k, d in enumerate((0, -1, 1)):
                mx(acc[:], b, q, W * (i0 + d + 1), UNIT, k == 0, k == 2)
            av = acc[:].rearrange("p (r m e) -> p r e m", m=32, e=2)[:, :, ::-1, :]
            dst = t_tiles[n % 4][:, q, :, 1:65].rearrange("p r (e m) -> p r e m", e=2)
            nc.scalar.activation(out=dst, in_=av, func=COPY, scale=NINTH)

        def border_row(n):
            b, u = where(n)
            side = 0 if u == 0 else 1
            eps = psume.tile([P, UNIT], F32, name="eps")
            for q in range(4):
                mx(eps[:, q * P:(q + 1) * P], b, q, W * (1 + side * 62), P, True, True)
            ev = eps[:].rearrange("p (q s m e) -> p q s e m", q=4, s=2, m=32, e=2)[:, :, side, ::-1, :]
            t_edge = edgep.tile([P, 4, SLOT], F32, name="t_edge")
            cc = (RHO - 1.0) * NINTH
            nc.scalar.activation(out=t_edge[:, :, 1:65].rearrange("p q (e m) -> p q e m", e=2), in_=ev, func=COPY, scale=cc)
            nc.scalar.activation(out=t_edge[:, :, 32:34], in_=t_edge[:, :, 32:34], func=COPY, scale=RHO)
            edge_of[n] = t_edge

        def weigh_ends(n, lo, hi):
            rows = t_tiles[n % 4][:].rearrange("p q r c -> p (q r) c")[:, lo:hi, 32:34]
            nc.scalar.activation(out=rows, in_=rows, func=COPY, scale=RHO)

        def add_border(n, q_lo, q_hi):
            b, u = where(n)
            r0 = 0 if u == 0 else UNIT_ROWS - 2
            t_tile = t_tiles[n % 4]
            nc.vector.tensor_tensor(
                out=t_tile[:, q_lo:q_hi, r0:r0 + 2, 1:65],
                in0=t_tile[:, q_lo:q_hi, r0:r0 + 2, 1:65],
                in1=edge_of[n][:, q_lo:q_hi, 1:65].unsqueeze(2).to_broadcast([P, q_hi - q_lo, 2, 64]),
                op=ADD,
            )

        def sum_rows(n, lo, hi):
            t_rows = t_tiles[n % 4][:].rearrange("p q r c -> p (q r) c")[:, lo:hi, :]
            pair = pairp.tile([P, hi - lo, 32], F32, name="pair%d" % (hi - lo))
            nc.vector.tensor_tensor(out=pair[:], in0=t_rows[:, :, 33:65], in1=t_rows[:, :, 1:33], op=ADD)
            nc.vector.tensor_tensor(
                out=y_of[n].rearrange("p q (r m e) -> p (q r) m e", m=32, e=2)[:, lo:hi, :, :],
                in0=t_rows.rearrange("p r (e y) -> p r y e", e=2)[:, :, 0:32, :],
                in1=pair[:].unsqueeze(3).to_broadcast([P, hi - lo, 32, 2]),
                op=ADD,
            )

        def scale_ends(n, lo, hi):
            if hi - lo == 32:
                ends = y_tiles[n % N_Y][:, Y_AT - 1:Y_AT - 1 + 33 * W].rearrange("p (k j) -> p k j", j=W)[:, :, 0:2]
            else:
                ends = y_of[n].rearrange("p q (r j) -> p (q r) j", j=W)[:, lo:hi, 0:W:W - 1]
            nc.scalar.activation(out=ends, in_=ends, func=COPY, scale=RHO)

        def scale_border(n, q_lo, q_hi):
            b, u = where(n)
            lo = 0 if u == 0 else (UNIT_ROWS - 1) * W
            row = y_of[n][:, q_lo:q_hi, lo:lo + W]
            nc.scalar.activation(out=row, in_=row, func=COPY, scale=RHO)

        def store(n, q_lo, q_hi):
            b, u = where(n)
            ob = out[b].rearrange("(q p) i j -> p q (i j)", p=P)
            nc.sync.dma_start(
                out=ob[:, q_lo:q_hi, u * UNIT:(u + 1) * UNIT],
                in_=y_of[n][:, q_lo:q_hi, :],
            )

        def new_y(n):
            y_of[n] = y_tiles[n % N_Y][:, Y_AT:Y_AT + 4 * UNIT].rearrange("p (q w) -> p q w", q=4)

        def fine_group(n):
            b, u = where(n)
            new_y(n)
            border_row(n)
            for q in range(4):
                lo = q * UNIT_ROWS
                bank(n, q)
                weigh_ends(n, lo, lo + UNIT_ROWS)
                add_border(n, q, q + 1)
                sum_rows(n, lo, lo + UNIT_ROWS)
                scale_ends(n, lo, lo + UNIT_ROWS)
                scale_border(n, q, q + 1)
                store(n, q, q + 1)

        def multiply_and_empty(n):
            b, u = where(n)
            for q in range(4):
                bank(n, q)
            weigh_ends(n, 0, 32)
            if u in (0, UNITS - 1):
                border_row(n)

        def add_up(n):
            b, u = where(n)
            if u in (0, UNITS - 1):
                add_border(n, 0, 4)
            new_y(n)
            sum_rows(n, 0, 32)

        def finish(n):
            b, u = where(n)
            scale_ends(n, 0, 32)
            if u in (0, UNITS - 1):
                scale_border(n, 0, 4)
            store(n, 0, 4)

        regroup(0)
        nc.vector.quantize_mx(
            out=w_codes[:].bitcast(FP8X4),
            scales=w_scales[:],
            in_=w_grp[:].rearrange("p w t -> p (w t)"),
        )
        for gu in range(1, RG_AHEAD):
            regroup(gu)
            if gu - 1 < Q_AHEAD:
                quantise(gu - 1)
        for gu in range(RG_AHEAD - 1, Q_AHEAD):
            quantise(gu)
        for n in range(N_GROUPS + 1):
            if n < N_GROUPS:
                if n in FINE_GROUPS:
                    fine_group(n)
                else:
                    multiply_and_empty(n)
            if n + RG_AHEAD < N_UNITS:
                regroup(n + RG_AHEAD)
            if n >= 1 and n - 1 not in FINE_GROUPS:
                add_up(n - 1)
            if n + Q_AHEAD < N_UNITS:
                quantise(n + Q_AHEAD)
            if n >= 1 and n - 1 not in FINE_GROUPS:
                finish(n - 1)
